import numpy as np
import ml_dtypes


def mxq(x, axis, fmt="e4m3"):
    dtype, down = {"e4m3": (ml_dtypes.float8_e4m3fn, 7), "e5m2": (ml_dtypes.float8_e5m2, 14)}[fmt]
    v = np.moveaxis(np.asarray(x, np.float32).astype(ml_dtypes.bfloat16).astype(np.float64), axis, -1)
    blocks = v.reshape(v.shape[:-1] + (-1, 32))
    amax = np.abs(blocks).max(-1, keepdims=True)
    byte = np.maximum(np.where(amax > 0, np.frexp(amax)[1] - 1 + 127, 0) - down, 1)
    scale = np.exp2(byte - 127.0)
    codes = (blocks / scale).astype(np.float32).astype(dtype).astype(np.float64)
    return np.moveaxis((codes * scale).reshape(v.shape), -1, axis)


WIDE = False


def mx_kscale(k):
    if not WIDE:
        return np.ones(k)
    levels = np.array([10, -10, 5, -5, 0])
    if k % 512:
        return np.exp2(np.random.permutation(np.resize(levels, k // 32))).repeat(32)
    a = np.empty((k // 512, 16))
    for p in range(k // 512):
        a[p, :8] = np.random.permutation(np.resize(levels, 8))
        for g in range(8):
            far = levels[np.abs(levels - a[p, g]) >= 10]
            a[p, g + 8] = far[np.random.randint(len(far))]
    return np.exp2(a.ravel()).repeat(32)


BF16 = ml_dtypes.bfloat16


def bf(x):
    return np.asarray(x, np.float32).astype(BF16)


def f64(x):
    return np.asarray(x).astype(np.float64)


M, K, N = 1536, 1536, 1536


def setup_inputs():
    s = mx_kscale(K)
    return {"A": bf(np.random.standard_normal((M, K)) * s),
            "B": bf(np.random.standard_normal((K, N)) * 2.0 / np.sqrt(K) / s[:, None])}


def reference(A, B):
    C = mxq(np.tril(f64(A)), 1, "e4m3") @ mxq(np.tril(f64(B)), 0, "e4m3")
    return np.tril(C)

@@ -1,0 +1,274 @@
+from contextlib import ExitStack
+
+import concourse.mybir as mybir
+from concourse.masks import make_identity
+
+BF16 = mybir.dt.bfloat16
+F32 = mybir.dt.float32
+I32 = mybir.dt.int32
+U32 = mybir.dt.uint32
+U8 = mybir.dt.uint8
+FP8X4 = mybir.dt.float8_e4m3fn_x4
+ALU = mybir.AluOpType
+
+SIZE = 1536
+P = 128
+K_PASS = 4 * P
+PASSES = SIZE // K_PASS
+STRIPE = 2 * P
+STRIPES = SIZE // STRIPE
+ROW_BLOCKS = SIZE // P
+
+FLOPS = 2 * (SIZE * (SIZE + 1) * (SIZE + 2) // 6)
+BYTES = 2 * (SIZE * (SIZE + 1) // 2) * 2 + SIZE * SIZE * 4
+
+
+def last_pass(s):
+    return STRIPE * s // K_PASS
+
+
+def tile_modelnew_kernel(tc, A, B, out):
+    nc = tc.nc
+    with ExitStack() as ctx:
+        const = ctx.enter_context(tc.tile_pool(name="const", bufs=1))
+        keep = ctx.enter_context(tc.tile_pool(name="keep", bufs=1))
+        stage_b = ctx.enter_context(tc.tile_pool(name="stage_b", bufs=3))
+        stage_a = ctx.enter_context(tc.tile_pool(name="stage_a", bufs=6))
+        psum = ctx.enter_context(tc.psum_pool(name="psum", bufs=8))
+        ctx.enter_context(tc.manual_schedule())
+
+        raw_a = []
+        for block in range(ROW_BLOCKS):
+            width = K_PASS * (block * P // K_PASS + 1)
+            raw_a.append(keep.tile([P, width], BF16, name="raw_a%d" % block, align_bytes=64))
+        raw_b = []
+        codes_b = []
+        scales_b = []
+        for c in range(PASSES):
+            width = K_PASS * (c + 1)
+            raw_b.append(keep.tile([P, 4, width], BF16, name="raw_b%d" % c, align_bytes=64))
+            codes_b.append(keep.tile([P, width], U32, name="codes_b%d" % c, align_bytes=64))
+            scales_b.append(keep.tile([P, width], U8, name="scales_b%d" % c, align_bytes=64))
+        pieces = [(s, c) for s in range(STRIPES) for c in range(last_pass(s) + 1)]
+        piece_of = dict((piece, i) for i, piece in enumerate(pieces))
+        codes_a = keep.tile([P, len(pieces), 2, P], U32, name="codes_a", align_bytes=64)
+        scales_a = keep.tile([P, len(pieces), 2, P], U8, name="scales_a", align_bytes=64)
+        out_sb = [keep.tile([P, 2, SIZE], F32, name="out_sb%d" % s) for s in range(4)]
+        out_sb.extend(out_sb[0:2])
+        ident = const.tile([P, P], F32, name="ident")
+        zero_src = const.tile([P, 8], F32, name="zero_src")
+        mask_a_f = const.tile([P, P // 2], F32, name="mask_a_f")
+        mask_b_f = const.tile([P, 4, K_PASS // 2], F32, name="mask_b_f")
+        mask_a = const.tile([P, P // 2], I32, name="mask_a")
+        mask_b = const.tile([P, 4, K_PASS // 2], I32, name="mask_b")
+        grouped_b = {}
+        grouped_a = {}
+        banks_t = {}
+        banks_o = {}
+
+
+        def load_b(c):
+            rows = B[K_PASS * c : K_PASS * (c + 1), 0 : K_PASS * (c + 1)]
+            nc.sync.dma_start(out=raw_b[c][:], in_=rows.rearrange("(p t) w -> p t w", t=4))
+
+        def load_a(block):
+            cols = P * (block + 1)
+            nc.sync.dma_start(
+                out=raw_a[block][:, 0:cols], in_=A[P * block : P * (block + 1), 0:cols]
+            )
+
+        def store(s):
+            rows = out[STRIPE * s : STRIPE * (s + 1), :].rearrange("(m j) n -> m j n", j=2)
+            nc.sync.dma_start(out=rows, in_=out_sb[s][:])
+
+
+        def build_masks():
+            nc.gpsimd.memset(mask_b_f[:], -1.0)
+            for base, fill in ((-1, 65535.0), (0, 0.0)):
+                nc.gpsimd.affine_select(
+                    out=mask_b_f[:], in_=mask_b_f[:], compare_op=ALU.is_ge, fill=fill,
+                    base=base, pattern=[[1, 4], [-2, K_PASS // 2]], channel_multiplier=4,
+                )
+            nc.gpsimd.memset(mask_a_f[:], -1.0)
+            for base, fill in ((-1, 65535.0), (0, 0.0)):
+                nc.gpsimd.affine_select(
+                    out=mask_a_f[:], in_=mask_a_f[:], compare_op=ALU.is_ge, fill=fill,
+                    base=base, pattern=[[-2, P // 2]], channel_multiplier=1,
+                )
+            make_identity(nc, ident[:])
+
+        def zero_a(block):
+            if P * (block + 1) % K_PASS:
+                nc.vector.memset(raw_a[block][:].bitcast(I32)[:, P * (block + 1) // 2 :], 0)
+
+        def zero_out_on_scalar(s):
+            for j in range(2):
+                kept = STRIPE * (s + 1)
+                nc.scalar.copy(
+                    out=out_sb[s][:, j, kept:],
+                    in_=zero_src[:, 0:1].to_broadcast([P, SIZE - kept]),
+                )
+
+        def zero_out_on_vector(s):
+            nc.vector.memset(out_sb[s][:, :, STRIPE * (s + 1) :], 0.0)
+
+        def mask_b_pass(c):
+            diag = raw_b[c][:].bitcast(I32)[:, :, K_PASS * c // 2 : K_PASS * (c + 1) // 2]
+            nc.vector.tensor_tensor(out=diag, in0=diag, in1=mask_b[:], op=ALU.bitwise_and)
+
+        def mask_a_stripe(s):
+            for block in (2 * s, 2 * s + 1):
+                zero_a(block)
+            for block in (2 * s, 2 * s + 1):
+                diag = raw_a[block][:].bitcast(I32)[:, P * block // 2 : P * (block + 1) // 2]
+                nc.vector.tensor_tensor(out=diag, in0=diag, in1=mask_a[:], op=ALU.bitwise_and)
+
+
+        def regroup_b(c, n):
+            cols = slice(K_PASS * n, K_PASS * (n + 1))
+            grouped = stage_b.tile([P, 4 * K_PASS], BF16, name="grouped_b", align_bytes=64)
+            grouped_b[(c, n)] = grouped
+            nc.vector.tensor_copy(
+                out=grouped[:].rearrange("p (w i t) -> p w t i", i=4, t=4),
+                in_=raw_b[c][:, :, cols].rearrange("p t (w i) -> p w t i", i=4),
+            )
+
+        def quantise_b(c, n):
+            cols = slice(K_PASS * n, K_PASS * (n + 1))
+            nc.vector.quantize_mx(
+                out=codes_b[c][:, cols].bitcast(FP8X4),
+                scales=scales_b[c][:, cols],
+                in_=grouped_b[(c, n)][:],
+            )
+
+
+        def transpose_a(s, c):
+            xt = psum.tile([P, 2, 2, P], F32, name="xt", tag="bank")
+            banks_t[(s, c)] = xt
+            for a in range(2):
+                a_words = raw_a[2 * s + a][:].bitcast(F32)
+                for u in range(2):
+                    lo, hi = K_PASS * c // 2, K_PASS * (c + 1) // 2
+                    nc.tensor.transpose(xt[:, u, a, :], a_words[:, lo + u : hi : 2], ident[:])
+            grouped = stage_a.tile([P, 2 * K_PASS], BF16, name="grouped_a", align_bytes=64)
+            grouped_a[(s, c)] = grouped
+            nc.scalar.copy(
+                out=grouped[:].bitcast(F32).rearrange("p (j m u) -> p j m u", j=2, u=2),
+                in_=xt[:].rearrange("p u a (x j) -> p j (a x) u", j=2),
+            )
+
+        def quantise_a(s, c):
+            i = piece_of[(s, c)]
+            nc.vector.quantize_mx(
+                out=codes_a[:, i, :, :].rearrange("p j m -> p (j m)").bitcast(FP8X4),
+                scales=scales_a[:, i, :, :].rearrange("p j m -> p (j m)"),
+                in_=grouped_a[(s, c)][:],
+            )
+
+
+        def width_of(s, n):
+            return min(K_PASS, STRIPE * (s + 1) - K_PASS * n)
+
+        def multiply(s, j, n, first, last):
+            if first == n:
+                acc = psum.tile([P, K_PASS], F32, name="acc", tag="bank")
+                banks_o[(s, j, n)] = acc
+            cols = slice(K_PASS * n, K_PASS * n + width_of(s, n))
+            for c in range(first, last + 1):
+                i = piece_of[(s, c)]
+                nc.tensor.matmul_mx(
+                    out=banks_o[(s, j, n)][:, 0 : width_of(s, n)],
+                    lhsT=codes_a[:, i, j, :].bitcast(FP8X4),
+                    lhsT_scale=scales_a[:, i, j, :],
+                    rhs=codes_b[c][:, cols].bitcast(FP8X4),
+                    rhs_scale=scales_b[c][:, cols],
+                    start=(c == n),
+                    stop=(c == last_pass(s)),
+                )
+
+        def copy_out(s, j, n, engine):
+            wide = width_of(s, n)
+            dst = out_sb[s][:, j, K_PASS * n : K_PASS * n + wide]
+            if engine == "vector":
+                nc.vector.tensor_copy(out=dst, in_=banks_o[(s, j, n)][:, 0:wide])
+            else:
+                nc.scalar.copy(out=dst, in_=banks_o[(s, j, n)][:, 0:wide])
+
+        def finish(s, first, on_vector=()):
+            for n in range(last_pass(s) + 1):
+                for j in range(2):
+                    multiply(s, j, n, max(first, n), last_pass(s))
+                    copy_out(s, j, n, "vector" if (j, n) in on_vector else "scalar")
+            store(s)
+
+        def start_early(s):
+            for n in range(last_pass(s)):
+                for j in range(2):
+                    multiply(s, j, n, n, last_pass(s) - 1)
+
+        load_b(0)
+        for block in range(0, 4):
+            load_a(block)
+        load_b(1)
+        for block in range(4, ROW_BLOCKS):
+            load_a(block)
+        load_b(2)
+
+        nc.vector.memset(zero_src[:], 0.0)
+        build_masks()
+        zero_out_on_scalar(0)
+        zero_out_on_scalar(1)
+        nc.vector.tensor_copy(out=mask_b[:], in_=mask_b_f[:])
+        zero_out_on_vector(2)
+        zero_out_on_vector(3)
+
+        mask_b_pass(0)
+        regroup_b(0, 0)
+        nc.vector.tensor_copy(out=mask_a[:], in_=mask_a_f[:])
+        mask_a_stripe(0)
+        mask_a_stripe(1)
+        quantise_b(0, 0)
+        transpose_a(0, 0)
+        transpose_a(1, 0)
+        mask_b_pass(1)
+        regroup_b(1, 0)
+        quantise_a(0, 0)
+        quantise_a(1, 0)
+        finish(0, 0)
+        finish(1, 0)
+
+        regroup_b(1, 1)
+        mask_a_stripe(2)
+        mask_a_stripe(3)
+        quantise_b(1, 0)
+        quantise_b(1, 1)
+        for s in (2, 3):
+            for c in range(2):
+                transpose_a(s, c)
+        mask_a_stripe(4)
+        mask_a_stripe(5)
+        for s in (2, 3):
+            for c in range(2):
+                quantise_a(s, c)
+        for c in range(PASSES):
+            transpose_a(4, c)
+        finish(2, 0)
+        finish(3, 0)
+        for c in range(PASSES):
+            transpose_a(5, c)
+
+        quantise_a(4, 0)
+        quantise_a(4, 1)
+        mask_b_pass(2)
+        regroup_b(2, 0)
+        quantise_a(4, 2)
+        regroup_b(2, 1)
+        quantise_b(2, 0)
+        regroup_b(2, 2)
+        quantise_b(2, 1)
+        quantise_b(2, 2)
+        for c in range(PASSES):
+            quantise_a(5, c)
+        start_early(4)
+        finish(4, 2, on_vector=((0, 2), (1, 2)))
+        finish(5, 0, on_vector=((1, 0), (1, 1), (1, 2)))

@@ -38,15 +38,21 @@ def tile_modelnew_kernel(tc, A, B, out):
         ctx.enter_context(tc.manual_schedule())
 
         raw_a = []
-        for block in range(ROW_BLOCKS):
-            width = K_PASS * (block * P // K_PASS + 1)
-            raw_a.append(keep.tile([P, width], BF16, name="raw_a%d" % block, align_bytes=64))
+        width_a = []
+        for s in range(STRIPES):
+            width = K_PASS * (last_pass(s) + 1)
+            width_a.append(width)
+            raw_a.append(
+                keep.tile([P, 2 * (width + 2 * P)], BF16, name="raw_a%d" % s, align_bytes=64)
+            )
         raw_b = []
+        kept_b = []
         codes_b = []
         scales_b = []
         for c in range(PASSES):
             width = K_PASS * (c + 1)
             raw_b.append(keep.tile([P, 4, width], BF16, name="raw_b%d" % c, align_bytes=64))
+            kept_b.append(keep.tile([P, 4, K_PASS], BF16, name="kept_b%d" % c, align_bytes=64))
             codes_b.append(keep.tile([P, width], U32, name="codes_b%d" % c, align_bytes=64))
             scales_b.append(keep.tile([P, width], U8, name="scales_b%d" % c, align_bytes=64))
         pieces = [(s, c) for s in range(STRIPES) for c in range(last_pass(s) + 1)]
@@ -57,9 +63,9 @@ def tile_modelnew_kernel(tc, A, B, out):
         out_sb.extend(out_sb[0:2])
         ident = const.tile([P, P], F32, name="ident")
         zero_src = const.tile([P, 8], F32, name="zero_src")
-        mask_a_f = const.tile([P, P // 2], F32, name="mask_a_f")
+        mask_a_f = const.tile([P, 2, P // 2], F32, name="mask_a_f")
         mask_b_f = const.tile([P, 4, K_PASS // 2], F32, name="mask_b_f")
-        mask_a = const.tile([P, P // 2], I32, name="mask_a")
+        mask_a = const.tile([P, 2, P // 2], I32, name="mask_a")
         mask_b = const.tile([P, 4, K_PASS // 2], I32, name="mask_b")
         grouped_b = {}
         grouped_a = {}
@@ -71,10 +77,15 @@ def tile_modelnew_kernel(tc, A, B, out):
             rows = B[K_PASS * c : K_PASS * (c + 1), 0 : K_PASS * (c + 1)]
             nc.sync.dma_start(out=raw_b[c][:], in_=rows.rearrange("(p t) w -> p t w", t=4))
 
+        def block_a(block, first, last):
+            s, a = divmod(block, 2)
+            start = a * (width_a[s] + P)
+            return raw_a[s][:, start + first : start + last]
+
         def load_a(block):
             cols = P * (block + 1)
             nc.sync.dma_start(
-                out=raw_a[block][:, 0:cols], in_=A[P * block : P * (block + 1), 0:cols]
+                out=block_a(block, 0, cols), in_=A[P * block : P * (block + 1), 0:cols]
             )
 
         def store(s):
@@ -82,63 +93,88 @@ def tile_modelnew_kernel(tc, A, B, out):
             nc.sync.dma_start(out=rows, in_=out_sb[s][:])
 
 
-        def build_masks():
-            nc.gpsimd.memset(mask_b_f[:], -1.0)
+        def ones():
+            nc.vector.memset(mask_b_f[:, :, 0:P], -1.0)
+            nc.vector.memset(mask_a_f[:], -1.0)
+
+        def build_mask_b(h):
+            cols = mask_b_f[:, :, P * h : P * (h + 1)]
             for base, fill in ((-1, 65535.0), (0, 0.0)):
                 nc.gpsimd.affine_select(
-                    out=mask_b_f[:], in_=mask_b_f[:], compare_op=ALU.is_ge, fill=fill,
-                    base=base, pattern=[[1, 4], [-2, K_PASS // 2]], channel_multiplier=4,
+                    out=cols, in_=cols, compare_op=ALU.is_ge, fill=fill,
+                    base=base - STRIPE * h, pattern=[[1, 4], [-2, P]], channel_multiplier=4,
                 )
-            nc.gpsimd.memset(mask_a_f[:], -1.0)
+
+        def convert_mask_b(h):
+            cols = slice(P * h, P * (h + 1))
+            nc.vector.tensor_copy(out=mask_b[:, :, cols], in_=mask_b_f[:, :, cols])
+
+        def build_masks():
+            build_mask_b(0)
+            make_identity(nc, ident[:])
             for base, fill in ((-1, 65535.0), (0, 0.0)):
                 nc.gpsimd.affine_select(
                     out=mask_a_f[:], in_=mask_a_f[:], compare_op=ALU.is_ge, fill=fill,
-                    base=base, pattern=[[-2, P // 2]], channel_multiplier=1,
+                    base=base, pattern=[[0, 2], [-2, P // 2]], channel_multiplier=1,
                 )
-            make_identity(nc, ident[:])
+            for block in range(4):
+                zero_a(block)
+            nc.gpsimd.memset(mask_b_f[:, :, P:], -1.0)
+            build_mask_b(1)
+            for block in range(4, ROW_BLOCKS):
+                zero_a(block)
 
         def zero_a(block):
-            if P * (block + 1) % K_PASS:
-                nc.vector.memset(raw_a[block][:].bitcast(I32)[:, P * (block + 1) // 2 :], 0)
+            width = width_a[block // 2]
+            if P * (block + 1) < width:
+                nc.gpsimd.memset(block_a(block, P * (block + 1), width).bitcast(I32), 0)
 
-        def zero_out_on_scalar(s):
-            for j in range(2):
-                kept = STRIPE * (s + 1)
-                nc.scalar.copy(
-                    out=out_sb[s][:, j, kept:],
-                    in_=zero_src[:, 0:1].to_broadcast([P, SIZE - kept]),
-                )
+        def zero_out_on_scalar(s, j):
+            kept = STRIPE * (s + 1)
+            nc.scalar.copy(
+                out=out_sb[s][:, j, kept:],
+                in_=zero_src[:, 0:1].to_broadcast([P, SIZE - kept]),
+            )
 
         def zero_out_on_vector(s):
             nc.vector.memset(out_sb[s][:, :, STRIPE * (s + 1) :], 0.0)
 
-        def mask_b_pass(c):
+        def mask_b_half(c, h):
+            half = slice(P * h, P * (h + 1))
             diag = raw_b[c][:].bitcast(I32)[:, :, K_PASS * c // 2 : K_PASS * (c + 1) // 2]
-            nc.vector.tensor_tensor(out=diag, in0=diag, in1=mask_b[:], op=ALU.bitwise_and)
-
-        def mask_a_stripe(s):
-            for block in (2 * s, 2 * s + 1):
-                zero_a(block)
-            for block in (2 * s, 2 * s + 1):
-                diag = raw_a[block][:].bitcast(I32)[:, P * block // 2 : P * (block + 1) // 2]
-                nc.vector.tensor_tensor(out=diag, in0=diag, in1=mask_a[:], op=ALU.bitwise_and)
-
-
-        def regroup_b(c, n):
-            cols = slice(K_PASS * n, K_PASS * (n + 1))
-            grouped = stage_b.tile([P, 4 * K_PASS], BF16, name="grouped_b", align_bytes=64)
-            grouped_b[(c, n)] = grouped
-            nc.vector.tensor_copy(
-                out=grouped[:].rearrange("p (w i t) -> p w t i", i=4, t=4),
-                in_=raw_b[c][:, :, cols].rearrange("p t (w i) -> p w t i", i=4),
+            nc.vector.tensor_tensor(
+                out=kept_b[c][:].bitcast(I32)[:, :, half], in0=diag[:, :, half],
+                in1=mask_b[:, :, half], op=ALU.bitwise_and,
             )
 
-        def quantise_b(c, n):
-            cols = slice(K_PASS * n, K_PASS * (n + 1))
+        def mask_b_pass(c):
+            diag = raw_b[c][:].bitcast(I32)[:, :, K_PASS * c // 2 : K_PASS * (c + 1) // 2]
+            nc.vector.tensor_tensor(
+                out=kept_b[c][:].bitcast(I32), in0=diag, in1=mask_b[:], op=ALU.bitwise_and
+            )
+
+        def mask_a_stripe(s):
+            both = raw_a[s][:].bitcast(I32).rearrange("p (a x) -> p a x", a=2)
+            diag = both[:, :, STRIPE * s // 2 : (STRIPE * s + P) // 2]
+            nc.vector.tensor_tensor(out=diag, in0=diag, in1=mask_a[:], op=ALU.bitwise_and)
+
+
+        def regroup_b(c, lo, hi, copy=nc.vector.tensor_copy):
+            rows, first = (kept_b[c], K_PASS * c) if lo >= K_PASS * c else (raw_b[c], 0)
+            cols = slice(lo - first, hi - first)
+            grouped = stage_b.tile([P, 4 * (hi - lo)], BF16, name="grouped_b", align_bytes=64)
+            grouped_b[(c, lo)] = grouped
+            copy(
+                out=grouped[:].rearrange("p (w i t) -> p w t i", i=4, t=4),
+                in_=rows[:, :, cols].rearrange("p t (w i) -> p w t i", i=4),
+            )
+
+        def quantise_b(c, lo, hi):
+            cols = slice(lo, hi)
             nc.vector.quantize_mx(
                 out=codes_b[c][:, cols].bitcast(FP8X4),
                 scales=scales_b[c][:, cols],
-                in_=grouped_b[(c, n)][:],
+                in_=grouped_b[(c, lo)][:],
             )
 
 
@@ -146,10 +182,9 @@ def tile_modelnew_kernel(tc, A, B, out):
             xt = psum.tile([P, 2, 2, P], F32, name="xt", tag="bank")
             banks_t[(s, c)] = xt
             for a in range(2):
-                a_words = raw_a[2 * s + a][:].bitcast(F32)
+                words = block_a(2 * s + a, K_PASS * c, K_PASS * (c + 1)).bitcast(F32)
                 for u in range(2):
-                    lo, hi = K_PASS * c // 2, K_PASS * (c + 1) // 2
-                    nc.tensor.transpose(xt[:, u, a, :], a_words[:, lo + u : hi : 2], ident[:])
+                    nc.tensor.transpose(xt[:, u, a, :], words[:, u::2], ident[:])
             grouped = stage_a.tile([P, 2 * K_PASS], BF16, name="grouped_a", align_bytes=64)
             grouped_a[(s, c)] = grouped
             nc.scalar.copy(
@@ -201,10 +236,13 @@ def tile_modelnew_kernel(tc, A, B, out):
                     copy_out(s, j, n, "vector" if (j, n) in on_vector else "scalar")
             store(s)
 
-        def start_early(s):
-            for n in range(last_pass(s)):
-                for j in range(2):
-                    multiply(s, j, n, n, last_pass(s) - 1)
+        def finish_tile(s, n):
+            for j in range(2):
+                multiply(s, j, n, n, last_pass(s))
+                copy_out(s, j, n, "vector" if j else "scalar")
+
+        def tile_of(n):
+            return K_PASS * n, K_PASS * (n + 1)
 
         load_b(0)
         for block in range(0, 4):
@@ -215,41 +253,49 @@ def tile_modelnew_kernel(tc, A, B, out):
         load_b(2)
 
         nc.vector.memset(zero_src[:], 0.0)
+        ones()
         build_masks()
-        zero_out_on_scalar(0)
-        zero_out_on_scalar(1)
-        nc.vector.tensor_copy(out=mask_b[:], in_=mask_b_f[:])
-        zero_out_on_vector(2)
+        zero_out_on_scalar(0, 0)
+        zero_out_on_scalar(0, 1)
+        zero_out_on_scalar(1, 0)
+        nc.gpsimd.memset(out_sb[1][:, 1, 2 * STRIPE :], 0.0)
         zero_out_on_vector(3)
+        convert_mask_b(0)
+        zero_out_on_vector(2)
 
-        mask_b_pass(0)
-        regroup_b(0, 0)
+        mask_b_half(0, 0)
+        regroup_b(0, 0, STRIPE)
         nc.vector.tensor_copy(out=mask_a[:], in_=mask_a_f[:])
         mask_a_stripe(0)
+        convert_mask_b(1)
         mask_a_stripe(1)
-        quantise_b(0, 0)
+        quantise_b(0, 0, STRIPE)
+        mask_b_half(0, 1)
+        regroup_b(0, STRIPE, K_PASS)
         transpose_a(0, 0)
         transpose_a(1, 0)
-        mask_b_pass(1)
-        regroup_b(1, 0)
         quantise_a(0, 0)
+        quantise_b(0, STRIPE, K_PASS)
         quantise_a(1, 0)
+        regroup_b(1, *tile_of(0))
         finish(0, 0)
         finish(1, 0)
 
-        regroup_b(1, 1)
         mask_a_stripe(2)
         mask_a_stripe(3)
-        quantise_b(1, 0)
-        quantise_b(1, 1)
+        mask_b_pass(1)
+        quantise_b(1, *tile_of(0))
+        regroup_b(1, *tile_of(1))
         for s in (2, 3):
             for c in range(2):
                 transpose_a(s, c)
         mask_a_stripe(4)
+        quantise_a(2, 0)
+        quantise_b(1, *tile_of(1))
+        quantise_a(2, 1)
+        quantise_a(3, 0)
+        quantise_a(3, 1)
         mask_a_stripe(5)
-        for s in (2, 3):
-            for c in range(2):
-                quantise_a(s, c)
         for c in range(PASSES):
             transpose_a(4, c)
         finish(2, 0)
@@ -257,18 +303,21 @@ def tile_modelnew_kernel(tc, A, B, out):
         for c in range(PASSES):
             transpose_a(5, c)
 
+        regroup_b(2, *tile_of(0))
+        mask_b_pass(2)
         quantise_a(4, 0)
         quantise_a(4, 1)
-        mask_b_pass(2)
-        regroup_b(2, 0)
+        quantise_b(2, *tile_of(0))
+        regroup_b(2, *tile_of(1))
         quantise_a(4, 2)
-        regroup_b(2, 1)
-        quantise_b(2, 0)
-        regroup_b(2, 2)
-        quantise_b(2, 1)
-        quantise_b(2, 2)
-        for c in range(PASSES):
-            quantise_a(5, c)
-        start_early(4)
-        finish(4, 2, on_vector=((0, 2), (1, 2)))
-        finish(5, 0, on_vector=((1, 0), (1, 1), (1, 2)))
+        regroup_b(2, *tile_of(2))
+        quantise_b(2, *tile_of(1))
+        quantise_a(5, 0)
+        quantise_b(2, *tile_of(2))
+        quantise_a(5, 1)
+        quantise_a(5, 2)
+        for s, n in ((4, 0), (4, 1), (4, 2), (5, 0), (5, 1), (5, 2)):
+            finish_tile(s, n)
+            if (s, n) == (4, 2):
+                store(4)
+        store(5)

@@ -64,7 +64,7 @@ def tile_modelnew_kernel(tc, A, B, out):
         ident = const.tile([P, P], F32, name="ident")
         zero_src = const.tile([P, 8], F32, name="zero_src")
         mask_a_f = const.tile([P, 2, P // 2], F32, name="mask_a_f")
-        mask_b_f = const.tile([P, 4, K_PASS // 2], F32, name="mask_b_f")
+        edge_b = const.tile([P, 2, STRIPE + 2], F32, name="edge_b")
         mask_a = const.tile([P, 2, P // 2], I32, name="mask_a")
         mask_b = const.tile([P, 4, K_PASS // 2], I32, name="mask_b")
         grouped_b = {}
@@ -94,40 +94,35 @@ def tile_modelnew_kernel(tc, A, B, out):
 
 
         def ones():
-            nc.vector.memset(mask_b_f[:, :, 0:P], -1.0)
+            nc.vector.memset(edge_b[:], -1.0)
             nc.vector.memset(mask_a_f[:], -1.0)
 
-        def build_mask_b(h):
-            cols = mask_b_f[:, :, P * h : P * (h + 1)]
-            for base, fill in ((-1, 65535.0), (0, 0.0)):
-                nc.gpsimd.affine_select(
-                    out=cols, in_=cols, compare_op=ALU.is_ge, fill=fill,
-                    base=base - STRIPE * h, pattern=[[1, 4], [-2, P]], channel_multiplier=4,
+        def expand_mask_b():
+            for h in range(2):
+                nc.vector.tensor_copy(
+                    out=mask_b[:, 2 * h : 2 * h + 2, :], in_=edge_b[:, :, 1 - h : 1 - h + STRIPE]
                 )
 
-        def convert_mask_b(h):
-            cols = slice(P * h, P * (h + 1))
-            nc.vector.tensor_copy(out=mask_b[:, :, cols], in_=mask_b_f[:, :, cols])
-
         def build_masks():
-            build_mask_b(0)
+            nc.gpsimd.affine_select(
+                out=edge_b[:, 0, :], in_=edge_b[:, 0, :], compare_op=ALU.is_ge, fill=65535.0,
+                base=1, pattern=[[-2, STRIPE + 2]], channel_multiplier=4,
+            )
+            nc.gpsimd.affine_select(
+                out=edge_b[:], in_=edge_b[:], compare_op=ALU.is_ge, fill=0.0,
+                base=2, pattern=[[0, 2], [-2, STRIPE + 2]], channel_multiplier=4,
+            )
             make_identity(nc, ident[:])
             for base, fill in ((-1, 65535.0), (0, 0.0)):
                 nc.gpsimd.affine_select(
                     out=mask_a_f[:], in_=mask_a_f[:], compare_op=ALU.is_ge, fill=fill,
                     base=base, pattern=[[0, 2], [-2, P // 2]], channel_multiplier=1,
                 )
-            for block in range(4):
-                zero_a(block)
-            nc.gpsimd.memset(mask_b_f[:, :, P:], -1.0)
-            build_mask_b(1)
-            for block in range(4, ROW_BLOCKS):
-                zero_a(block)
 
         def zero_a(block):
             width = width_a[block // 2]
             if P * (block + 1) < width:
-                nc.gpsimd.memset(block_a(block, P * (block + 1), width).bitcast(I32), 0)
+                nc.vector.memset(block_a(block, P * (block + 1), width).bitcast(I32), 0)
 
         def zero_out_on_scalar(s, j):
             kept = STRIPE * (s + 1)
@@ -236,11 +231,6 @@ def tile_modelnew_kernel(tc, A, B, out):
                     copy_out(s, j, n, "vector" if (j, n) in on_vector else "scalar")
             store(s)
 
-        def finish_tile(s, n):
-            for j in range(2):
-                multiply(s, j, n, n, last_pass(s))
-                copy_out(s, j, n, "vector" if j else "scalar")
-
         def tile_of(n):
             return K_PASS * n, K_PASS * (n + 1)
 
@@ -255,25 +245,25 @@ def tile_modelnew_kernel(tc, A, B, out):
         nc.vector.memset(zero_src[:], 0.0)
         ones()
         build_masks()
-        zero_out_on_scalar(0, 0)
-        zero_out_on_scalar(0, 1)
-        zero_out_on_scalar(1, 0)
-        nc.gpsimd.memset(out_sb[1][:, 1, 2 * STRIPE :], 0.0)
+        for s in range(2):
+            for j in range(2):
+                zero_out_on_scalar(s, j)
         zero_out_on_vector(3)
-        convert_mask_b(0)
-        zero_out_on_vector(2)
+        expand_mask_b()
+        nc.vector.tensor_copy(out=mask_a[:], in_=mask_a_f[:])
+        for block in range(ROW_BLOCKS):
+            zero_a(block)
 
         mask_b_half(0, 0)
-        regroup_b(0, 0, STRIPE)
-        nc.vector.tensor_copy(out=mask_a[:], in_=mask_a_f[:])
         mask_a_stripe(0)
-        convert_mask_b(1)
+        regroup_b(0, 0, STRIPE)
         mask_a_stripe(1)
-        quantise_b(0, 0, STRIPE)
         mask_b_half(0, 1)
+        quantise_b(0, 0, STRIPE)
         regroup_b(0, STRIPE, K_PASS)
         transpose_a(0, 0)
         transpose_a(1, 0)
+        zero_out_on_scalar(2, 0)
         quantise_a(0, 0)
         quantise_b(0, STRIPE, K_PASS)
         quantise_a(1, 0)
@@ -289,6 +279,7 @@ def tile_modelnew_kernel(tc, A, B, out):
         for s in (2, 3):
             for c in range(2):
                 transpose_a(s, c)
+        zero_out_on_scalar(2, 1)
         mask_a_stripe(4)
         quantise_a(2, 0)
         quantise_b(1, *tile_of(1))
@@ -315,9 +306,6 @@ def tile_modelnew_kernel(tc, A, B, out):
         quantise_a(5, 0)
         quantise_b(2, *tile_of(2))
         quantise_a(5, 1)
+        finish(4, 0, on_vector=((1, 2),))
         quantise_a(5, 2)
-        for s, n in ((4, 0), (4, 1), (4, 2), (5, 0), (5, 1), (5, 2)):
-            finish_tile(s, n)
-            if (s, n) == (4, 2):
-                store(4)
-        store(5)
+        finish(5, 0, on_vector=((1, 0), (1, 1), (1, 2)))

@@ -231,6 +231,19 @@ def tile_modelnew_kernel(tc, A, B, out):
                     copy_out(s, j, n, "vector" if (j, n) in on_vector else "scalar")
             store(s)
 
+        def start_early(s):
+            for n in range(last_pass(s)):
+                for j in range(2):
+                    multiply(s, j, n, n, last_pass(s) - 1)
+
+        def finish_by_parity(s):
+            for j in range(2):
+                for n in range(last_pass(s) + 1):
+                    multiply(s, j, n, n, last_pass(s))
+                    copy_out(s, j, n, "vector" if n == 1 else "scalar")
+                rows = out[STRIPE * s : STRIPE * (s + 1), :].rearrange("(m j) n -> m j n", j=2)
+                nc.sync.dma_start(out=rows[:, j, :], in_=out_sb[s][:, j, :])
+
         def tile_of(n):
             return K_PASS * n, K_PASS * (n + 1)
 
@@ -306,6 +319,7 @@ def tile_modelnew_kernel(tc, A, B, out):
         quantise_a(5, 0)
         quantise_b(2, *tile_of(2))
         quantise_a(5, 1)
-        finish(4, 0, on_vector=((1, 2),))
         quantise_a(5, 2)
-        finish(5, 0, on_vector=((1, 0), (1, 1), (1, 2)))
+        start_early(4)
+        finish(4, 2, on_vector=((1, 2),))
+        finish_by_parity(5)

@@ -39,11 +39,11 @@ def tile_modelnew_kernel(tc, A, B, out):
 
         raw_a = []
         width_a = []
-        for s in range(STRIPES):
-            width = K_PASS * (last_pass(s) + 1)
+        for g in range(PASSES):
+            width = K_PASS * (g + 1)
             width_a.append(width)
             raw_a.append(
-                keep.tile([P, 2 * (width + 2 * P)], BF16, name="raw_a%d" % s, align_bytes=64)
+                keep.tile([P, 4 * (width + 2 * P)], BF16, name="raw_a%d" % g, align_bytes=64)
             )
         raw_b = []
         kept_b = []
@@ -56,6 +56,7 @@ def tile_modelnew_kernel(tc, A, B, out):
             codes_b.append(keep.tile([P, width], U32, name="codes_b%d" % c, align_bytes=64))
             scales_b.append(keep.tile([P, width], U8, name="scales_b%d" % c, align_bytes=64))
         pieces = [(s, c) for s in range(STRIPES) for c in range(last_pass(s) + 1)]
+        runs = [(0, 2), (2, 2), (4, 2), (6, 2), (8, 1), (9, 2), (11, 1)]
         piece_of = dict((piece, i) for i, piece in enumerate(pieces))
         codes_a = keep.tile([P, len(pieces), 2, P], U32, name="codes_a", align_bytes=64)
         scales_a = keep.tile([P, len(pieces), 2, P], U8, name="scales_a", align_bytes=64)
@@ -63,9 +64,9 @@ def tile_modelnew_kernel(tc, A, B, out):
         out_sb.extend(out_sb[0:2])
         ident = const.tile([P, P], F32, name="ident")
         zero_src = const.tile([P, 8], F32, name="zero_src")
-        mask_a_f = const.tile([P, 2, P // 2], F32, name="mask_a_f")
+        mask_a_f = const.tile([P, P // 2], F32, name="mask_a_f")
         edge_b = const.tile([P, 2, STRIPE + 2], F32, name="edge_b")
-        mask_a = const.tile([P, 2, P // 2], I32, name="mask_a")
+        mask_a = const.tile([P, 4, P // 2], I32, name="mask_a")
         mask_b = const.tile([P, 4, K_PASS // 2], I32, name="mask_b")
         grouped_b = {}
         grouped_a = {}
@@ -78,9 +79,9 @@ def tile_modelnew_kernel(tc, A, B, out):
             nc.sync.dma_start(out=raw_b[c][:], in_=rows.rearrange("(p t) w -> p t w", t=4))
 
         def block_a(block, first, last):
-            s, a = divmod(block, 2)
-            start = a * (width_a[s] + P)
-            return raw_a[s][:, start + first : start + last]
+            g, i = divmod(block, 4)
+            start = i * (width_a[g] + P)
+            return raw_a[g][:, start + first : start + last]
 
         def load_a(block):
             cols = P * (block + 1)
@@ -116,11 +117,11 @@ def tile_modelnew_kernel(tc, A, B, out):
             for base, fill in ((-1, 65535.0), (0, 0.0)):
                 nc.gpsimd.affine_select(
                     out=mask_a_f[:], in_=mask_a_f[:], compare_op=ALU.is_ge, fill=fill,
-                    base=base, pattern=[[0, 2], [-2, P // 2]], channel_multiplier=1,
+                    base=base, pattern=[[-2, P // 2]], channel_multiplier=1,
                 )
 
         def zero_a(block):
-            width = width_a[block // 2]
+            width = width_a[block // 4]
             if P * (block + 1) < width:
                 nc.vector.memset(block_a(block, P * (block + 1), width).bitcast(I32), 0)
 
@@ -148,9 +149,9 @@ def tile_modelnew_kernel(tc, A, B, out):
                 out=kept_b[c][:].bitcast(I32), in0=diag, in1=mask_b[:], op=ALU.bitwise_and
             )
 
-        def mask_a_stripe(s):
-            both = raw_a[s][:].bitcast(I32).rearrange("p (a x) -> p a x", a=2)
-            diag = both[:, :, STRIPE * s // 2 : (STRIPE * s + P) // 2]
+        def mask_a_pair(g):
+            blocks = raw_a[g][:].bitcast(I32).rearrange("p (i x) -> p i x", i=4)
+            diag = blocks[:, :, K_PASS * g // 2 : (K_PASS * g + P) // 2]
             nc.vector.tensor_tensor(out=diag, in0=diag, in1=mask_a[:], op=ALU.bitwise_and)
 
 
@@ -173,6 +174,11 @@ def tile_modelnew_kernel(tc, A, B, out):
             )
 
 
+        def run_of(i):
+            for first, count in runs:
+                if first <= i < first + count:
+                    return first, count
+
         def transpose_a(s, c):
             xt = psum.tile([P, 2, 2, P], F32, name="xt", tag="bank")
             banks_t[(s, c)] = xt
@@ -180,19 +186,24 @@ def tile_modelnew_kernel(tc, A, B, out):
                 words = block_a(2 * s + a, K_PASS * c, K_PASS * (c + 1)).bitcast(F32)
                 for u in range(2):
                     nc.tensor.transpose(xt[:, u, a, :], words[:, u::2], ident[:])
-            grouped = stage_a.tile([P, 2 * K_PASS], BF16, name="grouped_a", align_bytes=64)
-            grouped_a[(s, c)] = grouped
+            i = piece_of[(s, c)]
+            first, count = run_of(i)
+            if i == first:
+                grouped_a[i] = stage_a.tile(
+                    [P, count, 2 * K_PASS], BF16, name="grouped_a", align_bytes=64
+                )
+            grouped = grouped_a[first][:, i - first, :]
             nc.scalar.copy(
-                out=grouped[:].bitcast(F32).rearrange("p (j m u) -> p j m u", j=2, u=2),
+                out=grouped.bitcast(F32).rearrange("p (j m u) -> p j m u", j=2, u=2),
                 in_=xt[:].rearrange("p u a (x j) -> p j (a x) u", j=2),
             )
 
-        def quantise_a(s, c):
-            i = piece_of[(s, c)]
+        def quantise_a(i):
+            count = run_of(i)[1]
             nc.vector.quantize_mx(
-                out=codes_a[:, i, :, :].rearrange("p j m -> p (j m)").bitcast(FP8X4),
-                scales=scales_a[:, i, :, :].rearrange("p j m -> p (j m)"),
-                in_=grouped_a[(s, c)][:],
+                out=codes_a[:, i : i + count].rearrange("p i j m -> p (i j m)").bitcast(FP8X4),
+                scales=scales_a[:, i : i + count].rearrange("p i j m -> p (i j m)"),
+                in_=grouped_a[i][:].rearrange("p i k -> p (i k)"),
             )
 
 
@@ -263,29 +274,27 @@ def tile_modelnew_kernel(tc, A, B, out):
                 zero_out_on_scalar(s, j)
         zero_out_on_vector(3)
         expand_mask_b()
-        nc.vector.tensor_copy(out=mask_a[:], in_=mask_a_f[:])
+        for i in range(4):
+            nc.vector.tensor_copy(out=mask_a[:, i, :], in_=mask_a_f[:])
         for block in range(ROW_BLOCKS):
             zero_a(block)
 
         mask_b_half(0, 0)
-        mask_a_stripe(0)
+        mask_a_pair(0)
         regroup_b(0, 0, STRIPE)
-        mask_a_stripe(1)
         mask_b_half(0, 1)
         quantise_b(0, 0, STRIPE)
         regroup_b(0, STRIPE, K_PASS)
         transpose_a(0, 0)
         transpose_a(1, 0)
         zero_out_on_scalar(2, 0)
-        quantise_a(0, 0)
+        quantise_a(0)
         quantise_b(0, STRIPE, K_PASS)
-        quantise_a(1, 0)
         regroup_b(1, *tile_of(0))
         finish(0, 0)
         finish(1, 0)
 
-        mask_a_stripe(2)
-        mask_a_stripe(3)
+        mask_a_pair(1)
         mask_b_pass(1)
         quantise_b(1, *tile_of(0))
         regroup_b(1, *tile_of(1))
@@ -293,13 +302,10 @@ def tile_modelnew_kernel(tc, A, B, out):
             for c in range(2):
                 transpose_a(s, c)
         zero_out_on_scalar(2, 1)
-        mask_a_stripe(4)
-        quantise_a(2, 0)
+        mask_a_pair(2)
+        quantise_a(2)
         quantise_b(1, *tile_of(1))
-        quantise_a(2, 1)
-        quantise_a(3, 0)
-        quantise_a(3, 1)
-        mask_a_stripe(5)
+        quantise_a(4)
         for c in range(PASSES):
             transpose_a(4, c)
         finish(2, 0)
@@ -309,17 +315,15 @@ def tile_modelnew_kernel(tc, A, B, out):
 
         regroup_b(2, *tile_of(0))
         mask_b_pass(2)
-        quantise_a(4, 0)
-        quantise_a(4, 1)
+        quantise_a(6)
         quantise_b(2, *tile_of(0))
         regroup_b(2, *tile_of(1))
-        quantise_a(4, 2)
+        quantise_a(8)
         regroup_b(2, *tile_of(2))
         quantise_b(2, *tile_of(1))
-        quantise_a(5, 0)
         quantise_b(2, *tile_of(2))
-        quantise_a(5, 1)
-        quantise_a(5, 2)
+        quantise_a(9)
         start_early(4)
         finish(4, 2, on_vector=((1, 2),))
+        quantise_a(11)
         finish_by_parity(5)

from contextlib import ExitStack

import concourse.mybir as mybir
from concourse.masks import make_identity

BF16 = mybir.dt.bfloat16
F32 = mybir.dt.float32
I32 = mybir.dt.int32
U32 = mybir.dt.uint32
U8 = mybir.dt.uint8
FP8X4 = mybir.dt.float8_e4m3fn_x4
ALU = mybir.AluOpType

SIZE = 1536
P = 128
K_PASS = 4 * P
PASSES = SIZE // K_PASS
STRIPE = 2 * P
STRIPES = SIZE // STRIPE
ROW_BLOCKS = SIZE // P

FLOPS = 2 * (SIZE * (SIZE + 1) * (SIZE + 2) // 6)
BYTES = 2 * (SIZE * (SIZE + 1) // 2) * 2 + SIZE * SIZE * 4


def last_pass(s):
    return STRIPE * s // K_PASS


def tile_modelnew_kernel(tc, A, B, out):
    nc = tc.nc
    with ExitStack() as ctx:
        const = ctx.enter_context(tc.tile_pool(name="const", bufs=1))
        keep = ctx.enter_context(tc.tile_pool(name="keep", bufs=1))
        stage_b = ctx.enter_context(tc.tile_pool(name="stage_b", bufs=3))
        stage_a = ctx.enter_context(tc.tile_pool(name="stage_a", bufs=6))
        psum = ctx.enter_context(tc.psum_pool(name="psum", bufs=8))
        ctx.enter_context(tc.manual_schedule())

        raw_a = []
        width_a = []
        for g in range(PASSES):
            width = K_PASS * (g + 1)
            width_a.append(width)
            raw_a.append(
                keep.tile([P, 4 * (width + 2 * P)], BF16, name="raw_a%d" % g, align_bytes=64)
            )
        raw_b = []
        kept_b = []
        codes_b = []
        scales_b = []
        for c in range(PASSES):
            width = K_PASS * (c + 1)
            raw_b.append(keep.tile([P, 4, width], BF16, name="raw_b%d" % c, align_bytes=64))
            kept_b.append(keep.tile([P, 4, K_PASS], BF16, name="kept_b%d" % c, align_bytes=64))
            codes_b.append(keep.tile([P, width], U32, name="codes_b%d" % c, align_bytes=64))
            scales_b.append(keep.tile([P, width], U8, name="scales_b%d" % c, align_bytes=64))
        pieces = [(s, c) for s in range(STRIPES) for c in range(last_pass(s) + 1)]
        runs = [(0, 2), (2, 2), (4, 2), (6, 2), (8, 1), (9, 2), (11, 1)]
        piece_of = dict((piece, i) for i, piece in enumerate(pieces))
        codes_a = keep.tile([P, len(pieces), 2, P], U32, name="codes_a", align_bytes=64)
        scales_a = keep.tile([P, len(pieces), 2, P], U8, name="scales_a", align_bytes=64)
        out_sb = [keep.tile([P, 2, SIZE], F32, name="out_sb%d" % s) for s in range(4)]
        out_sb.extend(out_sb[0:2])
        ident = const.tile([P, P], F32, name="ident")
        zero_src = const.tile([P, 8], F32, name="zero_src")
        mask_a_f = const.tile([P, P // 2], F32, name="mask_a_f")
        edge_b = const.tile([P, 2, STRIPE + 2], F32, name="edge_b")
        mask_a = const.tile([P, 4, P // 2], I32, name="mask_a")
        mask_b = const.tile([P, 4, K_PASS // 2], I32, name="mask_b")
        grouped_b = {}
        grouped_a = {}
        banks_t = {}
        banks_o = {}


        def load_b(c):
            rows = B[K_PASS * c : K_PASS * (c + 1), 0 : K_PASS * (c + 1)]
            nc.sync.dma_start(out=raw_b[c][:], in_=rows.rearrange("(p t) w -> p t w", t=4))

        def block_a(block, first, last):
            g, i = divmod(block, 4)
            start = i * (width_a[g] + P)
            return raw_a[g][:, start + first : start + last]

        def load_a(block):
            cols = P * (block + 1)
            nc.sync.dma_start(
                out=block_a(block, 0, cols), in_=A[P * block : P * (block + 1), 0:cols]
            )

        def store(s):
            rows = out[STRIPE * s : STRIPE * (s + 1), :].rearrange("(m j) n -> m j n", j=2)
            nc.sync.dma_start(out=rows, in_=out_sb[s][:])


        def ones():
            nc.vector.memset(edge_b[:], -1.0)
            nc.vector.memset(mask_a_f[:], -1.0)

        def expand_mask_b():
            for h in range(2):
                nc.vector.tensor_copy(
                    out=mask_b[:, 2 * h : 2 * h + 2, :], in_=edge_b[:, :, 1 - h : 1 - h + STRIPE]
                )

        def build_masks():
            nc.gpsimd.affine_select(
                out=edge_b[:, 0, :], in_=edge_b[:, 0, :], compare_op=ALU.is_ge, fill=65535.0,
                base=1, pattern=[[-2, STRIPE + 2]], channel_multiplier=4,
            )
            nc.gpsimd.affine_select(
                out=edge_b[:], in_=edge_b[:], compare_op=ALU.is_ge, fill=0.0,
                base=2, pattern=[[0, 2], [-2, STRIPE + 2]], channel_multiplier=4,
            )
            make_identity(nc, ident[:])
            for base, fill in ((-1, 65535.0), (0, 0.0)):
                nc.gpsimd.affine_select(
                    out=mask_a_f[:], in_=mask_a_f[:], compare_op=ALU.is_ge, fill=fill,
                    base=base, pattern=[[-2, P // 2]], channel_multiplier=1,
                )

        def zero_a(block):
            width = width_a[block // 4]
            if P * (block + 1) < width:
                nc.vector.memset(block_a(block, P * (block + 1), width).bitcast(I32), 0)

        def zero_out_on_scalar(s, j):
            kept = STRIPE * (s + 1)
            nc.scalar.copy(
                out=out_sb[s][:, j, kept:],
                in_=zero_src[:, 0:1].to_broadcast([P, SIZE - kept]),
            )

        def zero_out_on_vector(s):
            nc.vector.memset(out_sb[s][:, :, STRIPE * (s + 1) :], 0.0)

        def mask_b_half(c, h):
            half = slice(P * h, P * (h + 1))
            diag = raw_b[c][:].bitcast(I32)[:, :, K_PASS * c // 2 : K_PASS * (c + 1) // 2]
            nc.vector.tensor_tensor(
                out=kept_b[c][:].bitcast(I32)[:, :, half], in0=diag[:, :, half],
                in1=mask_b[:, :, half], op=ALU.bitwise_and,
            )

        def mask_b_pass(c):
            diag = raw_b[c][:].bitcast(I32)[:, :, K_PASS * c // 2 : K_PASS * (c + 1) // 2]
            nc.vector.tensor_tensor(
                out=kept_b[c][:].bitcast(I32), in0=diag, in1=mask_b[:], op=ALU.bitwise_and
            )

        def mask_a_pair(g):
            blocks = raw_a[g][:].bitcast(I32).rearrange("p (i x) -> p i x", i=4)
            diag = blocks[:, :, K_PASS * g // 2 : (K_PASS * g + P) // 2]
            nc.vector.tensor_tensor(out=diag, in0=diag, in1=mask_a[:], op=ALU.bitwise_and)


        def regroup_b(c, lo, hi, copy=nc.vector.tensor_copy):
            rows, first = (kept_b[c], K_PASS * c) if lo >= K_PASS * c else (raw_b[c], 0)
            cols = slice(lo - first, hi - first)
            grouped = stage_b.tile([P, 4 * (hi - lo)], BF16, name="grouped_b", align_bytes=64)
            grouped_b[(c, lo)] = grouped
            copy(
                out=grouped[:].rearrange("p (w i t) -> p w t i", i=4, t=4),
                in_=rows[:, :, cols].rearrange("p t (w i) -> p w t i", i=4),
            )

        def quantise_b(c, lo, hi):
            cols = slice(lo, hi)
            nc.vector.quantize_mx(
                out=codes_b[c][:, cols].bitcast(FP8X4),
                scales=scales_b[c][:, cols],
                in_=grouped_b[(c, lo)][:],
            )


        def run_of(i):
            for first, count in runs:
                if first <= i < first + count:
                    return first, count

        def transpose_a(s, c):
            xt = psum.tile([P, 2, 2, P], F32, name="xt", tag="bank")
            banks_t[(s, c)] = xt
            for a in range(2):
                words = block_a(2 * s + a, K_PASS * c, K_PASS * (c + 1)).bitcast(F32)
                for u in range(2):
                    nc.tensor.transpose(xt[:, u, a, :], words[:, u::2], ident[:])
            i = piece_of[(s, c)]
            first, count = run_of(i)
            if i == first:
                grouped_a[i] = stage_a.tile(
                    [P, count, 2 * K_PASS], BF16, name="grouped_a", align_bytes=64
                )
            grouped = grouped_a[first][:, i - first, :]
            nc.scalar.copy(
                out=grouped.bitcast(F32).rearrange("p (j m u) -> p j m u", j=2, u=2),
                in_=xt[:].rearrange("p u a (x j) -> p j (a x) u", j=2),
            )

        def quantise_a(i):
            count = run_of(i)[1]
            nc.vector.quantize_mx(
                out=codes_a[:, i : i + count].rearrange("p i j m -> p (i j m)").bitcast(FP8X4),
                scales=scales_a[:, i : i + count].rearrange("p i j m -> p (i j m)"),
                in_=grouped_a[i][:].rearrange("p i k -> p (i k)"),
            )


        def width_of(s, n):
            return min(K_PASS, STRIPE * (s + 1) - K_PASS * n)

        def multiply(s, j, n, first, last):
            if first == n:
                acc = psum.tile([P, K_PASS], F32, name="acc", tag="bank")
                banks_o[(s, j, n)] = acc
            cols = slice(K_PASS * n, K_PASS * n + width_of(s, n))
            for c in range(first, last + 1):
                i = piece_of[(s, c)]
                nc.tensor.matmul_mx(
                    out=banks_o[(s, j, n)][:, 0 : width_of(s, n)],
                    lhsT=codes_a[:, i, j, :].bitcast(FP8X4),
                    lhsT_scale=scales_a[:, i, j, :],
                    rhs=codes_b[c][:, cols].bitcast(FP8X4),
                    rhs_scale=scales_b[c][:, cols],
                    start=(c == n),
                    stop=(c == last_pass(s)),
                )

        def copy_out(s, j, n, engine):
            wide = width_of(s, n)
            dst = out_sb[s][:, j, K_PASS * n : K_PASS * n + wide]
            if engine == "vector":
                nc.vector.tensor_copy(out=dst, in_=banks_o[(s, j, n)][:, 0:wide])
            else:
                nc.scalar.copy(out=dst, in_=banks_o[(s, j, n)][:, 0:wide])

        def finish(s, first, on_vector=()):
            for n in range(last_pass(s) + 1):
                for j in range(2):
                    multiply(s, j, n, max(first, n), last_pass(s))
                    copy_out(s, j, n, "vector" if (j, n) in on_vector else "scalar")
            store(s)

        def start_early(s):
            for n in range(last_pass(s)):
                for j in range(2):
                    multiply(s, j, n, n, last_pass(s) - 1)

        def finish_by_parity(s):
            for j in range(2):
                for n in range(last_pass(s) + 1):
                    multiply(s, j, n, n, last_pass(s))
                    copy_out(s, j, n, "vector" if n == 1 else "scalar")
                rows = out[STRIPE * s : STRIPE * (s + 1), :].rearrange("(m j) n -> m j n", j=2)
                nc.sync.dma_start(out=rows[:, j, :], in_=out_sb[s][:, j, :])

        def tile_of(n):
            return K_PASS * n, K_PASS * (n + 1)

        load_b(0)
        for block in range(0, 4):
            load_a(block)
        load_b(1)
        for block in range(4, ROW_BLOCKS):
            load_a(block)
        load_b(2)

        nc.vector.memset(zero_src[:], 0.0)
        ones()
        build_masks()
        for s in range(2):
            for j in range(2):
                zero_out_on_scalar(s, j)
        zero_out_on_vector(3)
        expand_mask_b()
        for i in range(4):
            nc.vector.tensor_copy(out=mask_a[:, i, :], in_=mask_a_f[:])
        for block in range(ROW_BLOCKS):
            zero_a(block)

        mask_b_half(0, 0)
        mask_a_pair(0)
        regroup_b(0, 0, STRIPE)
        mask_b_half(0, 1)
        quantise_b(0, 0, STRIPE)
        regroup_b(0, STRIPE, K_PASS)
        transpose_a(0, 0)
        transpose_a(1, 0)
        zero_out_on_scalar(2, 0)
        quantise_a(0)
        quantise_b(0, STRIPE, K_PASS)
        regroup_b(1, *tile_of(0))
        finish(0, 0)
        finish(1, 0)

        mask_a_pair(1)
        mask_b_pass(1)
        quantise_b(1, *tile_of(0))
        regroup_b(1, *tile_of(1))
        for s in (2, 3):
            for c in range(2):
                transpose_a(s, c)
        zero_out_on_scalar(2, 1)
        mask_a_pair(2)
        quantise_a(2)
        quantise_b(1, *tile_of(1))
        quantise_a(4)
        for c in range(PASSES):
            transpose_a(4, c)
        finish(2, 0)
        finish(3, 0)
        for c in range(PASSES):
            transpose_a(5, c)

        regroup_b(2, *tile_of(0))
        mask_b_pass(2)
        quantise_a(6)
        quantise_b(2, *tile_of(0))
        regroup_b(2, *tile_of(1))
        quantise_a(8)
        regroup_b(2, *tile_of(2))
        quantise_b(2, *tile_of(1))
        quantise_b(2, *tile_of(2))
        quantise_a(9)
        start_early(4)
        finish(4, 2, on_vector=((1, 2),))
        quantise_a(11)
        finish_by_parity(5)
